import numpy as np
import ml_dtypes


def mxq(x, axis, fmt="e4m3"):
    dtype, down = {"e4m3": (ml_dtypes.float8_e4m3fn, 7), "e5m2": (ml_dtypes.float8_e5m2, 14)}[fmt]
    v = np.moveaxis(np.asarray(x, np.float32).astype(ml_dtypes.bfloat16).astype(np.float64), axis, -1)
    blocks = v.reshape(v.shape[:-1] + (-1, 32))
    amax = np.abs(blocks).max(-1, keepdims=True)
    byte = np.maximum(np.where(amax > 0, np.frexp(amax)[1] - 1 + 127, 0) - down, 1)
    scale = np.exp2(byte - 127.0)
    codes = (blocks / scale).astype(np.float32).astype(dtype).astype(np.float64)
    return np.moveaxis((codes * scale).reshape(v.shape), -1, axis)


WIDE = False


def mx_kscale(k):
    if not WIDE:
        return np.ones(k)
    levels = np.array([10, -10, 5, -5, 0])
    if k % 512:
        return np.exp2(np.random.permutation(np.resize(levels, k // 32))).repeat(32)
    a = np.empty((k // 512, 16))
    for p in range(k // 512):
        a[p, :8] = np.random.permutation(np.resize(levels, 8))
        for g in range(8):
            far = levels[np.abs(levels - a[p, g]) >= 10]
            a[p, g + 8] = far[np.random.randint(len(far))]
    return np.exp2(a.ravel()).repeat(32)


BF16 = ml_dtypes.bfloat16


def bf(x):
    return np.asarray(x, np.float32).astype(BF16)


def f64(x):
    return np.asarray(x).astype(np.float64)


B, L, H, D = 2, 512, 8, 128
DIM = H * D


def setup_inputs():
    r = np.random.standard_normal
    s = mx_kscale(DIM)
    ang = np.arange(L)[:, None, None] * (r((H, D)) * 0.2)[None]
    return {"x": bf(r((B, L, DIM)) * s),
            "wq_w": bf(r((DIM, DIM)) * 0.5 / np.sqrt(DIM) / s[None, :]),
            "wq_b": bf(r(DIM) * 0.1),
            "wk_w": bf(r((DIM, DIM)) * 0.5 / np.sqrt(DIM) / s[None, :]),
            "wk_b": bf(r(DIM) * 0.1),
            "rot_re": bf(np.cos(ang)),
            "rot_im": bf(np.sin(ang))}


def reference(x, wq_w, wq_b, wk_w, wk_b, rot_re, rot_im):
    xq = mxq(f64(x), 2, "e4m3")
    q = ((xq @ mxq(f64(wq_w), 1, "e4m3").T) + f64(wq_b)).reshape(B, L, H, D)
    k = ((xq @ mxq(f64(wk_w), 1, "e4m3").T) + f64(wk_b)).reshape(B, L, H, D)
    c = f64(rot_re)[None]
    sn = f64(rot_im)[None]
    return q * c, q * sn, k * c, -(k * sn)

@@ -1,0 +1,218 @@
+from contextlib import ExitStack
+
+import concourse.mybir as mybir
+from concourse.masks import make_identity
+
+F32 = mybir.dt.float32
+BF16 = mybir.dt.bfloat16
+U32 = mybir.dt.uint32
+U8 = mybir.dt.uint8
+FP8X4 = mybir.dt.float8_e4m3fn_x4
+MULT = mybir.AluOpType.mult
+IDENTITY = mybir.ActivationFunctionType.Identity
+
+P = 128
+BATCH = 2
+TOKENS = 512
+DIM = 1024
+TOKEN_TILES = TOKENS // P
+CHANNEL_TILES = DIM // P
+PASSES = DIM // (4 * P)
+BANK = 512
+
+BLOCK_ROWS = 2 * P
+BLOCK_VALUES = 4 * BLOCK_ROWS
+
+UNITS = 2 * BATCH * (TOKENS // BLOCK_ROWS)
+HALVES = 2 * UNITS
+MX_LAG = 4
+BACK_LAG = MX_LAG + 1
+
+FLOPS = 2 * BATCH * TOKENS * DIM * 2 * DIM
+
+
+def tile_retention_pa_kernel(
+    tc, x, wq_w, wq_b, wk_w, wk_b, rot_re, rot_im, out_0, out_1, out_2, out_3
+):
+    nc = tc.nc
+    with ExitStack() as ctx:
+        ctx.enter_context(tc.manual_schedule())
+        keep = ctx.enter_context(tc.tile_pool(name="keep", bufs=1))
+        grouped_pool = ctx.enter_context(tc.tile_pool(name="grouped", bufs=3))
+        biased_pool = ctx.enter_context(tc.tile_pool(name="biased", bufs=3 * 2))
+        result_pool = ctx.enter_context(tc.tile_pool(name="result", bufs=12))
+        scalar_banks = ctx.enter_context(tc.psum_pool(name="scalar_banks", bufs=4))
+        back_banks = ctx.enter_context(tc.psum_pool(name="back_banks", bufs=4))
+
+        x_rows = [x[b].rearrange("(p j) k -> p j k", j=TOKEN_TILES) for b in range(BATCH)]
+        w_rows = [w.rearrange("(i p r) k -> p i r k", p=P, r=2) for w in (wq_w, wk_w)]
+        rot_rows = [r.rearrange("(p j) h d -> p j (h d)", j=TOKEN_TILES) for r in (rot_re, rot_im)]
+        out_rows = [
+            [
+                [o[b].rearrange("(p j) h d -> p j (h d)", j=TOKEN_TILES) for b in range(BATCH)]
+                for o in pair
+            ]
+            for pair in ((out_0, out_1), (out_2, out_3))
+        ]
+
+        x_codes = [keep.tile([P, PASSES, TOKENS], U32, align_bytes=64, name="x_codes%d" % b) for b in range(BATCH)]
+        x_scales = [keep.tile([P, PASSES, TOKENS], U8, align_bytes=64, name="x_scales%d" % b) for b in range(BATCH)]
+        w_codes = [keep.tile([P, PASSES, DIM], U32, align_bytes=64, name="w_codes%d" % i) for i in range(2)]
+        w_scales = [keep.tile([P, PASSES, DIM], U8, align_bytes=64, name="w_scales%d" % i) for i in range(2)]
+
+        x_blocks = [
+            (x_rows[b][:, 2 * i : 2 * i + 2, :], x_codes[b], x_scales[b], i * BLOCK_ROWS, "k r c u")
+            for b in range(BATCH)
+            for i in range(TOKENS // BLOCK_ROWS)
+        ]
+        w_blocks = [
+            [
+                (w_rows[proj][:, i, :, :], w_codes[proj], w_scales[proj], i * BLOCK_ROWS, "k c r u")
+                for i in range(DIM // BLOCK_ROWS)
+            ]
+            for proj in range(2)
+        ]
+        blocks = x_blocks[0:1] + w_blocks[0] + x_blocks[1:] + w_blocks[1]
+
+        def unit_parts(unit):
+            proj, x_block = divmod(unit, len(x_blocks))
+            b, token_pair = divmod(x_block, TOKENS // BLOCK_ROWS)
+            return proj, b, token_pair
+
+        bias_rows = keep.tile([P, P], BF16)
+        nc.vector.memset(bias_rows[:], 0.0)
+        nc.scalar.dma_start(out=bias_rows[0:CHANNEL_TILES, :], in_=wq_b.rearrange("(m p) -> m p", p=P))
+        nc.scalar.dma_start(
+            out=bias_rows[CHANNEL_TILES : 2 * CHANNEL_TILES, :], in_=wk_b.rearrange("(m p) -> m p", p=P)
+        )
+
+        rot_sb = keep.tile([P, 3, TOKEN_TILES, DIM], BF16)
+        tables_of = (slice(0, 2), slice(0, 3, 2))
+        raw_tiles = []
+        for i, block in enumerate(blocks):
+            raw = keep.tile([P, 2 * DIM], BF16, name="raw%d" % i)
+            nc.sync.dma_start(out=raw[:].rearrange("p (r k) -> p r k", r=2), in_=block[0])
+            raw_tiles.append(raw)
+            if i - BACK_LAG in range(0, TOKEN_TILES, 2):
+                tiles = slice(i - BACK_LAG, i - BACK_LAG + 2)
+                for part in range(2):
+                    nc.sync.dma_start(out=rot_sb[:, part, tiles, :], in_=rot_rows[part][:, tiles, :])
+
+        ident = keep.tile([P, P], F32)
+        make_identity(nc, ident[:])
+
+        bias_col = keep.tile([P, 2 * CHANNEL_TILES], F32)
+
+        def spread_bias():
+            bias_rows_f32 = keep.tile([P, P], F32)
+            nc.vector.tensor_copy(out=bias_rows_f32[:], in_=bias_rows[:])
+            bias_bank = scalar_banks.tile([P, 4, P], F32, tag="bank")
+            nc.tensor.transpose(out=bias_bank[:, 0, :], in_=bias_rows_f32[:], identity=ident[:])
+            nc.vector.tensor_copy(out=bias_col[:], in_=bias_bank[:, 0, 0 : 2 * CHANNEL_TILES])
+
+        def transpose_in(i, vector_is_idle):
+            column_order = blocks[i][4]
+            raw_words = raw_tiles[i][:].bitcast(F32).rearrange("p (r w) -> p r w", r=2)
+            grouped = grouped_pool.tile([P, PASSES * BLOCK_VALUES], BF16, align_bytes=64, tag="grouped")
+            grouped_words = grouped[:].bitcast(F32).rearrange("k (g w) -> k g w", g=PASSES)
+            for g in range(PASSES):
+                bank = scalar_banks.tile([P, 4, P], F32, tag="bank")
+                for r in range(2):
+                    for u in range(2):
+                        nc.tensor.transpose(
+                            out=bank[:, 2 * r + u, :],
+                            in_=raw_words[:, r, 2 * P * g + u : 2 * P * (g + 1) : 2],
+                            identity=ident[:],
+                        )
+                ordered = bank[:].rearrange("k (r u) c -> " + column_order, u=2)
+                target = grouped_words[:, g, :].rearrange("k (" + column_order[2:] + ") -> " + column_order, r=2, u=2)
+                if g == 1 and vector_is_idle:
+                    nc.vector.tensor_copy(out=target, in_=ordered)
+                else:
+                    nc.scalar.copy(out=target, in_=ordered)
+            return grouped
+
+        def quantise(i, grouped):
+            codes, scales, first = blocks[i][1:4]
+            cols = slice(first, first + BLOCK_ROWS)
+            for g in range(PASSES):
+                nc.vector.quantize_mx(
+                    out=codes[:, g, cols].bitcast(FP8X4),
+                    scales=scales[:, g, cols],
+                    in_=grouped[:, g * BLOCK_VALUES : (g + 1) * BLOCK_VALUES],
+                )
+
+        biased = {}
+
+        def multiply(n):
+            unit, half = divmod(n, 2)
+            proj, b, token_pair = unit_parts(unit)
+            tokens = slice(token_pair * BLOCK_ROWS, (token_pair + 1) * BLOCK_ROWS)
+            for pair in (2 * half, 2 * half + 1):
+                acc = scalar_banks.tile([P, 2, BLOCK_ROWS], F32, tag="bank")
+                with_bias = biased_pool.tile([P, 2, BLOCK_ROWS], F32, tag="biased")
+                for i in range(2):
+                    m = 2 * pair + i
+                    channels = slice(m * P, (m + 1) * P)
+                    for g in range(PASSES):
+                        nc.tensor.matmul_mx(
+                            out=acc[:, i, :],
+                            lhsT=w_codes[proj][:, g, channels].bitcast(FP8X4),
+                            lhsT_scale=w_scales[proj][:, g, channels],
+                            rhs=x_codes[b][:, g, tokens].bitcast(FP8X4),
+                            rhs_scale=x_scales[b][:, g, tokens],
+                            start=(g == 0),
+                            stop=(g == PASSES - 1),
+                        )
+                for i in range(2):
+                    column = proj * CHANNEL_TILES + 2 * pair + i
+                    nc.scalar.activation(
+                        out=with_bias[:, i, :],
+                        in_=acc[:, i, :],
+                        func=IDENTITY,
+                        bias=bias_col[:, column : column + 1],
+                        scale=1.0,
+                    )
+                biased[(unit, pair)] = with_bias
+
+        def finish(n):
+            unit, half = divmod(n, 2)
+            proj, b, token_pair = unit_parts(unit)
+            cols = slice(half * BANK, (half + 1) * BANK)
+            banks = []
+            for tile_in_unit in range(2):
+                bank = back_banks.tile([P, 4, P], F32, tag="back")
+                for i in range(4):
+                    nc.tensor.transpose(
+                        out=bank[:, i, :],
+                        in_=biased[(unit, 2 * half + i // 2)][:, i % 2, tile_in_unit * P : (tile_in_unit + 1) * P],
+                        identity=ident[:],
+                    )
+                banks.append(bank)
+            for tile_in_unit, bank in enumerate(banks):
+                j = 2 * token_pair + tile_in_unit
+                product = bank[:].rearrange("p i c -> p (i c)").unsqueeze(1).to_broadcast([P, 2, BANK])
+                results = result_pool.tile([P, 2, BANK], F32, tag="results")
+                nc.vector.tensor_tensor(
+                    out=results[:], in0=product, in1=rot_sb[:, tables_of[proj], j, cols], op=MULT
+                )
+                for part in range(2):
+                    nc.sync.dma_start(out=out_rows[proj][part][b][:, j, cols], in_=results[:, part, :])
+
+        for slot in range(MX_LAG):
+            quantise(slot, transpose_in(slot, vector_is_idle=True))
+        spread_bias()
+        first_k_finish = HALVES // 2 + BACK_LAG
+        for slot in range(MX_LAG, HALVES + BACK_LAG):
+            if slot < len(blocks):
+                quantise(slot, transpose_in(slot, vector_is_idle=(slot < BACK_LAG)))
+            if slot - MX_LAG < HALVES:
+                multiply(slot - MX_LAG)
+            if slot >= BACK_LAG:
+                finish(slot - BACK_LAG)
+            piece = slot - (first_k_finish - 1)
+            if 0 <= piece < TOKEN_TILES:
+                token_pair, half = divmod(piece, 2)
+                tiles = slice(2 * token_pair, 2 * token_pair + 2)
+                cols = slice(half * BANK, (half + 1) * BANK)
+                nc.scalar.mul(rot_sb[:, 2, tiles, cols], rot_sb[:, 1, tiles, cols], -1.0)

@@ -23,8 +23,7 @@ BANK = 512
 BLOCK_ROWS = 2 * P
 BLOCK_VALUES = 4 * BLOCK_ROWS
 
-UNITS = 2 * BATCH * (TOKENS // BLOCK_ROWS)
-HALVES = 2 * UNITS
+UNITS = 2 * BATCH * TOKEN_TILES
 MX_LAG = 4
 BACK_LAG = MX_LAG + 1
 
@@ -40,7 +39,7 @@ def tile_retention_pa_kernel(
         keep = ctx.enter_context(tc.tile_pool(name="keep", bufs=1))
         grouped_pool = ctx.enter_context(tc.tile_pool(name="grouped", bufs=3))
         biased_pool = ctx.enter_context(tc.tile_pool(name="biased", bufs=3 * 2))
-        result_pool = ctx.enter_context(tc.tile_pool(name="result", bufs=12))
+        result_pool = ctx.enter_context(tc.tile_pool(name="result", bufs=7))
         scalar_banks = ctx.enter_context(tc.psum_pool(name="scalar_banks", bufs=4))
         back_banks = ctx.enter_context(tc.psum_pool(name="back_banks", bufs=4))
 
@@ -75,9 +74,9 @@ def tile_retention_pa_kernel(
         blocks = x_blocks[0:1] + w_blocks[0] + x_blocks[1:] + w_blocks[1]
 
         def unit_parts(unit):
-            proj, x_block = divmod(unit, len(x_blocks))
-            b, token_pair = divmod(x_block, TOKENS // BLOCK_ROWS)
-            return proj, b, token_pair
+            proj, x_tile = divmod(unit, BATCH * TOKEN_TILES)
+            b, j = divmod(x_tile, TOKEN_TILES)
+            return proj, b, j
 
         bias_rows = keep.tile([P, P], BF16)
         nc.vector.memset(bias_rows[:], 0.0)
@@ -144,15 +143,14 @@ def tile_retention_pa_kernel(
 
         biased = {}
 
-        def multiply(n):
-            unit, half = divmod(n, 2)
-            proj, b, token_pair = unit_parts(unit)
-            tokens = slice(token_pair * BLOCK_ROWS, (token_pair + 1) * BLOCK_ROWS)
-            for pair in (2 * half, 2 * half + 1):
-                acc = scalar_banks.tile([P, 2, BLOCK_ROWS], F32, tag="bank")
-                with_bias = biased_pool.tile([P, 2, BLOCK_ROWS], F32, tag="biased")
-                for i in range(2):
-                    m = 2 * pair + i
+        def multiply(unit):
+            proj, b, j = unit_parts(unit)
+            tokens = slice(j * P, (j + 1) * P)
+            for half in range(2):
+                acc = scalar_banks.tile([P, 4, P], F32, tag="bank")
+                with_bias = biased_pool.tile([P, 4, P], F32, tag="biased")
+                for i in range(4):
+                    m = 4 * half + i
                     channels = slice(m * P, (m + 1) * P)
                     for g in range(PASSES):
                         nc.tensor.matmul_mx(
@@ -164,8 +162,8 @@ def tile_retention_pa_kernel(
                             start=(g == 0),
                             stop=(g == PASSES - 1),
                         )
-                for i in range(2):
-                    column = proj * CHANNEL_TILES + 2 * pair + i
+                for i in range(4):
+                    column = proj * CHANNEL_TILES + 4 * half + i
                     nc.scalar.activation(
                         out=with_bias[:, i, :],
                         in_=acc[:, i, :],
@@ -173,46 +171,41 @@ def tile_retention_pa_kernel(
                         bias=bias_col[:, column : column + 1],
                         scale=1.0,
                     )
-                biased[(unit, pair)] = with_bias
+                biased[(unit, half)] = with_bias
 
-        def finish(n):
-            unit, half = divmod(n, 2)
-            proj, b, token_pair = unit_parts(unit)
-            cols = slice(half * BANK, (half + 1) * BANK)
+        def finish(unit):
+            proj, b, j = unit_parts(unit)
             banks = []
-            for tile_in_unit in range(2):
+            for half in range(2):
                 bank = back_banks.tile([P, 4, P], F32, tag="back")
                 for i in range(4):
-                    nc.tensor.transpose(
-                        out=bank[:, i, :],
-                        in_=biased[(unit, 2 * half + i // 2)][:, i % 2, tile_in_unit * P : (tile_in_unit + 1) * P],
-                        identity=ident[:],
-                    )
+                    nc.tensor.transpose(out=bank[:, i, :], in_=biased[(unit, half)][:, i, :], identity=ident[:])
                 banks.append(bank)
-            for tile_in_unit, bank in enumerate(banks):
-                j = 2 * token_pair + tile_in_unit
+            results = result_pool.tile([P, 2, DIM], F32, tag="results")
+            for half, bank in enumerate(banks):
+                cols = slice(half * BANK, (half + 1) * BANK)
                 product = bank[:].rearrange("p i c -> p (i c)").unsqueeze(1).to_broadcast([P, 2, BANK])
-                results = result_pool.tile([P, 2, BANK], F32, tag="results")
                 nc.vector.tensor_tensor(
-                    out=results[:], in0=product, in1=rot_sb[:, tables_of[proj], j, cols], op=MULT
+                    out=results[:, :, cols], in0=product, in1=rot_sb[:, tables_of[proj], j, cols], op=MULT
                 )
+                if unit == UNITS - 1:
+                    for part in range(2):
+                        nc.sync.dma_start(out=out_rows[proj][part][b][:, j, cols], in_=results[:, part, cols])
+            if unit < UNITS - 1:
                 for part in range(2):
-                    nc.sync.dma_start(out=out_rows[proj][part][b][:, j, cols], in_=results[:, part, :])
+                    nc.sync.dma_start(out=out_rows[proj][part][b][:, j, :], in_=results[:, part, :])
 
         for slot in range(MX_LAG):
             quantise(slot, transpose_in(slot, vector_is_idle=True))
         spread_bias()
-        first_k_finish = HALVES // 2 + BACK_LAG
-        for slot in range(MX_LAG, HALVES + BACK_LAG):
+        first_k_finish = UNITS // 2 + BACK_LAG
+        for slot in range(MX_LAG, UNITS + BACK_LAG):
             if slot < len(blocks):
                 quantise(slot, transpose_in(slot, vector_is_idle=(slot < BACK_LAG)))
-            if slot - MX_LAG < HALVES:
+            if slot - MX_LAG < UNITS:
                 multiply(slot - MX_LAG)
             if slot >= BACK_LAG:
                 finish(slot - BACK_LAG)
-            piece = slot - (first_k_finish - 1)
-            if 0 <= piece < TOKEN_TILES:
-                token_pair, half = divmod(piece, 2)
-                tiles = slice(2 * token_pair, 2 * token_pair + 2)
-                cols = slice(half * BANK, (half + 1) * BANK)
-                nc.scalar.mul(rot_sb[:, 2, tiles, cols], rot_sb[:, 1, tiles, cols], -1.0)
+            j = slot - (first_k_finish - 1)
+            if 0 <= j < TOKEN_TILES:
+                nc.scalar.mul(rot_sb[:, 2, j, :], rot_sb[:, 1, j, :], -1.0)

@@ -8,6 +8,7 @@ BF16 = mybir.dt.bfloat16
 U32 = mybir.dt.uint32
 U8 = mybir.dt.uint8
 FP8X4 = mybir.dt.float8_e4m3fn_x4
+ADD = mybir.AluOpType.add
 MULT = mybir.AluOpType.mult
 IDENTITY = mybir.ActivationFunctionType.Identity
 
@@ -39,7 +40,8 @@ def tile_retention_pa_kernel(
         keep = ctx.enter_context(tc.tile_pool(name="keep", bufs=1))
         grouped_pool = ctx.enter_context(tc.tile_pool(name="grouped", bufs=3))
         biased_pool = ctx.enter_context(tc.tile_pool(name="biased", bufs=3 * 2))
-        result_pool = ctx.enter_context(tc.tile_pool(name="result", bufs=7))
+        result_pool = ctx.enter_context(tc.tile_pool(name="result", bufs=8))
+        summed_pool = ctx.enter_context(tc.tile_pool(name="summed", bufs=3))
         scalar_banks = ctx.enter_context(tc.psum_pool(name="scalar_banks", bufs=4))
         back_banks = ctx.enter_context(tc.psum_pool(name="back_banks", bufs=4))
 
@@ -100,7 +102,11 @@ def tile_retention_pa_kernel(
         ident = keep.tile([P, P], F32)
         make_identity(nc, ident[:])
 
+        ident_bf16 = keep.tile([P, P], BF16)
+        make_identity(nc, ident_bf16[:])
+
         bias_col = keep.tile([P, 2 * CHANNEL_TILES], F32)
+        bias_all = keep.tile([P, BANK], BF16)
 
         def spread_bias():
             bias_rows_f32 = keep.tile([P, P], F32)
@@ -108,6 +114,16 @@ def tile_retention_pa_kernel(
             bias_bank = scalar_banks.tile([P, 4, P], F32, tag="bank")
             nc.tensor.transpose(out=bias_bank[:, 0, :], in_=bias_rows_f32[:], identity=ident[:])
             nc.vector.tensor_copy(out=bias_col[:], in_=bias_bank[:, 0, 0 : 2 * CHANNEL_TILES])
+            all_bank = scalar_banks.tile([P, 4, P], F32, tag="bank")
+            for m in range(4):
+                nc.tensor.matmul(
+                    out=all_bank[:, m, :],
+                    lhsT=ident_bf16[:, m : m + 1].to_broadcast([P, P]),
+                    rhs=bias_rows[:],
+                    start=True,
+                    stop=True,
+                )
+            nc.scalar.copy(out=bias_all[:], in_=all_bank[:].rearrange("p i c -> p (i c)"))
 
         def transpose_in(i, vector_is_idle):
             column_order = blocks[i][4]
@@ -142,11 +158,41 @@ def tile_retention_pa_kernel(
                 )
 
         biased = {}
+        unit_results = {}
+
+        def is_direct(unit, half):
+            return unit < UNITS // 2 and half == 0
+
+        def direct(unit):
+            proj, b, j = unit_parts(unit)
+            tokens = slice(j * P, (j + 1) * P)
+            acc = back_banks.tile([P, 4, P], F32, tag="back")
+            product = acc[:].rearrange("p i c -> p (i c)")
+            for g in range(PASSES):
+                nc.tensor.matmul_mx(
+                    out=product,
+                    lhsT=x_codes[b][:, g, tokens].bitcast(FP8X4),
+                    lhsT_scale=x_scales[b][:, g, tokens],
+                    rhs=w_codes[proj][:, g, 0:BANK].bitcast(FP8X4),
+                    rhs_scale=w_scales[proj][:, g, 0:BANK],
+                    start=(g == 0),
+                    stop=(g == PASSES - 1),
+                )
+            summed = summed_pool.tile([P, BANK], F32, tag="summed")
+            nc.vector.tensor_tensor(out=summed[:], in0=product, in1=bias_all[:], op=ADD)
+            for part in range(2):
+                nc.gpsimd.tensor_tensor(
+                    out=unit_results[unit][:, part, 0:BANK], in0=summed[:], in1=rot_sb[:, part, j, 0:BANK], op=MULT
+                )
 
         def multiply(unit):
             proj, b, j = unit_parts(unit)
             tokens = slice(j * P, (j + 1) * P)
+            unit_results[unit] = result_pool.tile([P, 2, DIM], F32, tag="results", name="results")
             for half in range(2):
+                if is_direct(unit, half):
+                    direct(unit)
+                    continue
                 acc = scalar_banks.tile([P, 4, P], F32, tag="bank")
                 with_bias = biased_pool.tile([P, 4, P], F32, tag="biased")
                 for i in range(4):
@@ -175,14 +221,16 @@ def tile_retention_pa_kernel(
 
         def finish(unit):
             proj, b, j = unit_parts(unit)
-            banks = []
+            banks = {}
             for half in range(2):
-                bank = back_banks.tile([P, 4, P], F32, tag="back")
-                for i in range(4):
-                    nc.tensor.transpose(out=bank[:, i, :], in_=biased[(unit, half)][:, i, :], identity=ident[:])
-                banks.append(bank)
-            results = result_pool.tile([P, 2, DIM], F32, tag="results")
-            for half, bank in enumerate(banks):
+                if not is_direct(unit, half):
+                    banks[half] = back_banks.tile([P, 4, P], F32, tag="back", name="back")
+                    for i in range(4):
+                        nc.tensor.transpose(
+                            out=banks[half][:, i, :], in_=biased[(unit, half)][:, i, :], identity=ident[:]
+                        )
+            results = unit_results[unit]
+            for half, bank in banks.items():
                 cols = slice(half * BANK, (half + 1) * BANK)
                 product = bank[:].rearrange("p i c -> p (i c)").unsqueeze(1).to_broadcast([P, 2, BANK])
                 nc.vector.tensor_tensor(

@@ -82,10 +82,13 @@ def tile_retention_pa_kernel(
 
         bias_rows = keep.tile([P, P], BF16)
         nc.vector.memset(bias_rows[:], 0.0)
-        nc.scalar.dma_start(out=bias_rows[0:CHANNEL_TILES, :], in_=wq_b.rearrange("(m p) -> m p", p=P))
-        nc.scalar.dma_start(
-            out=bias_rows[CHANNEL_TILES : 2 * CHANNEL_TILES, :], in_=wk_b.rearrange("(m p) -> m p", p=P)
-        )
+
+        def load_biases():
+            for proj, bias in enumerate((wq_b, wk_b)):
+                nc.sync.dma_start(
+                    out=bias_rows[proj * CHANNEL_TILES : (proj + 1) * CHANNEL_TILES, :],
+                    in_=bias.rearrange("(m p) -> m p", p=P),
+                )
 
         rot_sb = keep.tile([P, 3, TOKEN_TILES, DIM], BF16)
         tables_of = (slice(0, 2), slice(0, 3, 2))
@@ -94,6 +97,8 @@ def tile_retention_pa_kernel(
             raw = keep.tile([P, 2 * DIM], BF16, name="raw%d" % i)
             nc.sync.dma_start(out=raw[:].rearrange("p (r k) -> p r k", r=2), in_=block[0])
             raw_tiles.append(raw)
+            if i == 0:
+                load_biases()
             if i - BACK_LAG in range(0, TOKEN_TILES, 2):
                 tiles = slice(i - BACK_LAG, i - BACK_LAG + 2)
                 for part in range(2):
@@ -108,13 +113,14 @@ def tile_retention_pa_kernel(
         bias_col = keep.tile([P, 2 * CHANNEL_TILES], F32)
         bias_all = keep.tile([P, BANK], BF16)
 
+        bias_rows_f32 = keep.tile([P, P], F32)
+        nc.gpsimd.tensor_copy(out=bias_rows_f32[:], in_=bias_rows[:])
+
         def spread_bias():
-            bias_rows_f32 = keep.tile([P, P], F32)
-            nc.vector.tensor_copy(out=bias_rows_f32[:], in_=bias_rows[:])
-            bias_bank = scalar_banks.tile([P, 4, P], F32, tag="bank")
+            bias_bank = back_banks.tile([P, 4, P], F32, tag="back")
             nc.tensor.transpose(out=bias_bank[:, 0, :], in_=bias_rows_f32[:], identity=ident[:])
-            nc.vector.tensor_copy(out=bias_col[:], in_=bias_bank[:, 0, 0 : 2 * CHANNEL_TILES])
-            all_bank = scalar_banks.tile([P, 4, P], F32, tag="bank")
+            nc.scalar.copy(out=bias_col[:], in_=bias_bank[:, 0, 0 : 2 * CHANNEL_TILES])
+            all_bank = back_banks.tile([P, 4, P], F32, tag="back")
             for m in range(4):
                 nc.tensor.matmul(
                     out=all_bank[:, m, :],

@@ -225,6 +225,8 @@ def tile_retention_pa_kernel(
                     )
                 biased[(unit, half)] = with_bias
 
+        late_stores = []
+
         def finish(unit):
             proj, b, j = unit_parts(unit)
             banks = {}
@@ -246,8 +248,8 @@ def tile_retention_pa_kernel(
                     for part in range(2):
                         nc.sync.dma_start(out=out_rows[proj][part][b][:, j, cols], in_=results[:, part, cols])
             if unit < UNITS - 1:
-                for part in range(2):
-                    nc.sync.dma_start(out=out_rows[proj][part][b][:, j, :], in_=results[:, part, :])
+                nc.sync.dma_start(out=out_rows[proj][0][b][:, j, :], in_=results[:, 0, :])
+                late_stores.append((out_rows[proj][1][b][:, j, :], results[:, 1, :]))
 
         for slot in range(MX_LAG):
             quantise(slot, transpose_in(slot, vector_is_idle=True))
@@ -258,6 +260,9 @@ def tile_retention_pa_kernel(
                 quantise(slot, transpose_in(slot, vector_is_idle=(slot < BACK_LAG)))
             if slot - MX_LAG < UNITS:
                 multiply(slot - MX_LAG)
+            for target, source in late_stores:
+                nc.scalar.dma_start(out=target, in_=source)
+            late_stores.clear()
             if slot >= BACK_LAG:
                 finish(slot - BACK_LAG)
             j = slot - (first_k_finish - 1)

from contextlib import ExitStack

import concourse.mybir as mybir
from concourse.masks import make_identity

F32 = mybir.dt.float32
BF16 = mybir.dt.bfloat16
U32 = mybir.dt.uint32
U8 = mybir.dt.uint8
FP8X4 = mybir.dt.float8_e4m3fn_x4
ADD = mybir.AluOpType.add
MULT = mybir.AluOpType.mult
IDENTITY = mybir.ActivationFunctionType.Identity

P = 128
BATCH = 2
TOKENS = 512
DIM = 1024
TOKEN_TILES = TOKENS // P
CHANNEL_TILES = DIM // P
PASSES = DIM // (4 * P)
BANK = 512

BLOCK_ROWS = 2 * P
BLOCK_VALUES = 4 * BLOCK_ROWS

UNITS = 2 * BATCH * TOKEN_TILES
MX_LAG = 4
BACK_LAG = MX_LAG + 1

FLOPS = 2 * BATCH * TOKENS * DIM * 2 * DIM


def tile_retention_pa_kernel(
    tc, x, wq_w, wq_b, wk_w, wk_b, rot_re, rot_im, out_0, out_1, out_2, out_3
):
    nc = tc.nc
    with ExitStack() as ctx:
        ctx.enter_context(tc.manual_schedule())
        keep = ctx.enter_context(tc.tile_pool(name="keep", bufs=1))
        grouped_pool = ctx.enter_context(tc.tile_pool(name="grouped", bufs=3))
        biased_pool = ctx.enter_context(tc.tile_pool(name="biased", bufs=3 * 2))
        result_pool = ctx.enter_context(tc.tile_pool(name="result", bufs=8))
        summed_pool = ctx.enter_context(tc.tile_pool(name="summed", bufs=3))
        scalar_banks = ctx.enter_context(tc.psum_pool(name="scalar_banks", bufs=4))
        back_banks = ctx.enter_context(tc.psum_pool(name="back_banks", bufs=4))

        x_rows = [x[b].rearrange("(p j) k -> p j k", j=TOKEN_TILES) for b in range(BATCH)]
        w_rows = [w.rearrange("(i p r) k -> p i r k", p=P, r=2) for w in (wq_w, wk_w)]
        rot_rows = [r.rearrange("(p j) h d -> p j (h d)", j=TOKEN_TILES) for r in (rot_re, rot_im)]
        out_rows = [
            [
                [o[b].rearrange("(p j) h d -> p j (h d)", j=TOKEN_TILES) for b in range(BATCH)]
                for o in pair
            ]
            for pair in ((out_0, out_1), (out_2, out_3))
        ]

        x_codes = [keep.tile([P, PASSES, TOKENS], U32, align_bytes=64, name="x_codes%d" % b) for b in range(BATCH)]
        x_scales = [keep.tile([P, PASSES, TOKENS], U8, align_bytes=64, name="x_scales%d" % b) for b in range(BATCH)]
        w_codes = [keep.tile([P, PASSES, DIM], U32, align_bytes=64, name="w_codes%d" % i) for i in range(2)]
        w_scales = [keep.tile([P, PASSES, DIM], U8, align_bytes=64, name="w_scales%d" % i) for i in range(2)]

        x_blocks = [
            (x_rows[b][:, 2 * i : 2 * i + 2, :], x_codes[b], x_scales[b], i * BLOCK_ROWS, "k r c u")
            for b in range(BATCH)
            for i in range(TOKENS // BLOCK_ROWS)
        ]
        w_blocks = [
            [
                (w_rows[proj][:, i, :, :], w_codes[proj], w_scales[proj], i * BLOCK_ROWS, "k c r u")
                for i in range(DIM // BLOCK_ROWS)
            ]
            for proj in range(2)
        ]
        blocks = x_blocks[0:1] + w_blocks[0] + x_blocks[1:] + w_blocks[1]

        def unit_parts(unit):
            proj, x_tile = divmod(unit, BATCH * TOKEN_TILES)
            b, j = divmod(x_tile, TOKEN_TILES)
            return proj, b, j

        bias_rows = keep.tile([P, P], BF16)
        nc.vector.memset(bias_rows[:], 0.0)

        def load_biases():
            for proj, bias in enumerate((wq_b, wk_b)):
                nc.sync.dma_start(
                    out=bias_rows[proj * CHANNEL_TILES : (proj + 1) * CHANNEL_TILES, :],
                    in_=bias.rearrange("(m p) -> m p", p=P),
                )

        rot_sb = keep.tile([P, 3, TOKEN_TILES, DIM], BF16)
        tables_of = (slice(0, 2), slice(0, 3, 2))
        raw_tiles = []
        for i, block in enumerate(blocks):
            raw = keep.tile([P, 2 * DIM], BF16, name="raw%d" % i)
            nc.sync.dma_start(out=raw[:].rearrange("p (r k) -> p r k", r=2), in_=block[0])
            raw_tiles.append(raw)
            if i == 0:
                load_biases()
            if i - BACK_LAG in range(0, TOKEN_TILES, 2):
                tiles = slice(i - BACK_LAG, i - BACK_LAG + 2)
                for part in range(2):
                    nc.sync.dma_start(out=rot_sb[:, part, tiles, :], in_=rot_rows[part][:, tiles, :])

        ident = keep.tile([P, P], F32)
        make_identity(nc, ident[:])

        ident_bf16 = keep.tile([P, P], BF16)
        make_identity(nc, ident_bf16[:])

        bias_col = keep.tile([P, 2 * CHANNEL_TILES], F32)
        bias_all = keep.tile([P, BANK], BF16)

        bias_rows_f32 = keep.tile([P, P], F32)
        nc.gpsimd.tensor_copy(out=bias_rows_f32[:], in_=bias_rows[:])

        def spread_bias():
            bias_bank = back_banks.tile([P, 4, P], F32, tag="back")
            nc.tensor.transpose(out=bias_bank[:, 0, :], in_=bias_rows_f32[:], identity=ident[:])
            nc.scalar.copy(out=bias_col[:], in_=bias_bank[:, 0, 0 : 2 * CHANNEL_TILES])
            all_bank = back_banks.tile([P, 4, P], F32, tag="back")
            for m in range(4):
                nc.tensor.matmul(
                    out=all_bank[:, m, :],
                    lhsT=ident_bf16[:, m : m + 1].to_broadcast([P, P]),
                    rhs=bias_rows[:],
                    start=True,
                    stop=True,
                )
            nc.scalar.copy(out=bias_all[:], in_=all_bank[:].rearrange("p i c -> p (i c)"))

        def transpose_in(i, vector_is_idle):
            column_order = blocks[i][4]
            raw_words = raw_tiles[i][:].bitcast(F32).rearrange("p (r w) -> p r w", r=2)
            grouped = grouped_pool.tile([P, PASSES * BLOCK_VALUES], BF16, align_bytes=64, tag="grouped")
            grouped_words = grouped[:].bitcast(F32).rearrange("k (g w) -> k g w", g=PASSES)
            for g in range(PASSES):
                bank = scalar_banks.tile([P, 4, P], F32, tag="bank")
                for r in range(2):
                    for u in range(2):
                        nc.tensor.transpose(
                            out=bank[:, 2 * r + u, :],
                            in_=raw_words[:, r, 2 * P * g + u : 2 * P * (g + 1) : 2],
                            identity=ident[:],
                        )
                ordered = bank[:].rearrange("k (r u) c -> " + column_order, u=2)
                target = grouped_words[:, g, :].rearrange("k (" + column_order[2:] + ") -> " + column_order, r=2, u=2)
                if g == 1 and vector_is_idle:
                    nc.vector.tensor_copy(out=target, in_=ordered)
                else:
                    nc.scalar.copy(out=target, in_=ordered)
            return grouped

        def quantise(i, grouped):
            codes, scales, first = blocks[i][1:4]
            cols = slice(first, first + BLOCK_ROWS)
            for g in range(PASSES):
                nc.vector.quantize_mx(
                    out=codes[:, g, cols].bitcast(FP8X4),
                    scales=scales[:, g, cols],
                    in_=grouped[:, g * BLOCK_VALUES : (g + 1) * BLOCK_VALUES],
                )

        biased = {}
        unit_results = {}

        def is_direct(unit, half):
            return unit < UNITS // 2 and half == 0

        def direct(unit):
            proj, b, j = unit_parts(unit)
            tokens = slice(j * P, (j + 1) * P)
            acc = back_banks.tile([P, 4, P], F32, tag="back")
            product = acc[:].rearrange("p i c -> p (i c)")
            for g in range(PASSES):
                nc.tensor.matmul_mx(
                    out=product,
                    lhsT=x_codes[b][:, g, tokens].bitcast(FP8X4),
                    lhsT_scale=x_scales[b][:, g, tokens],
                    rhs=w_codes[proj][:, g, 0:BANK].bitcast(FP8X4),
                    rhs_scale=w_scales[proj][:, g, 0:BANK],
                    start=(g == 0),
                    stop=(g == PASSES - 1),
                )
            summed = summed_pool.tile([P, BANK], F32, tag="summed")
            nc.vector.tensor_tensor(out=summed[:], in0=product, in1=bias_all[:], op=ADD)
            for part in range(2):
                nc.gpsimd.tensor_tensor(
                    out=unit_results[unit][:, part, 0:BANK], in0=summed[:], in1=rot_sb[:, part, j, 0:BANK], op=MULT
                )

        def multiply(unit):
            proj, b, j = unit_parts(unit)
            tokens = slice(j * P, (j + 1) * P)
            unit_results[unit] = result_pool.tile([P, 2, DIM], F32, tag="results", name="results")
            for half in range(2):
                if is_direct(unit, half):
                    direct(unit)
                    continue
                acc = scalar_banks.tile([P, 4, P], F32, tag="bank")
                with_bias = biased_pool.tile([P, 4, P], F32, tag="biased")
                for i in range(4):
                    m = 4 * half + i
                    channels = slice(m * P, (m + 1) * P)
                    for g in range(PASSES):
                        nc.tensor.matmul_mx(
                            out=acc[:, i, :],
                            lhsT=w_codes[proj][:, g, channels].bitcast(FP8X4),
                            lhsT_scale=w_scales[proj][:, g, channels],
                            rhs=x_codes[b][:, g, tokens].bitcast(FP8X4),
                            rhs_scale=x_scales[b][:, g, tokens],
                            start=(g == 0),
                            stop=(g == PASSES - 1),
                        )
                for i in range(4):
                    column = proj * CHANNEL_TILES + 4 * half + i
                    nc.scalar.activation(
                        out=with_bias[:, i, :],
                        in_=acc[:, i, :],
                        func=IDENTITY,
                        bias=bias_col[:, column : column + 1],
                        scale=1.0,
                    )
                biased[(unit, half)] = with_bias

        late_stores = []

        def finish(unit):
            proj, b, j = unit_parts(unit)
            banks = {}
            for half in range(2):
                if not is_direct(unit, half):
                    banks[half] = back_banks.tile([P, 4, P], F32, tag="back", name="back")
                    for i in range(4):
                        nc.tensor.transpose(
                            out=banks[half][:, i, :], in_=biased[(unit, half)][:, i, :], identity=ident[:]
                        )
            results = unit_results[unit]
            for half, bank in banks.items():
                cols = slice(half * BANK, (half + 1) * BANK)
                product = bank[:].rearrange("p i c -> p (i c)").unsqueeze(1).to_broadcast([P, 2, BANK])
                nc.vector.tensor_tensor(
                    out=results[:, :, cols], in0=product, in1=rot_sb[:, tables_of[proj], j, cols], op=MULT
                )
                if unit == UNITS - 1:
                    for part in range(2):
                        nc.sync.dma_start(out=out_rows[proj][part][b][:, j, cols], in_=results[:, part, cols])
            if unit < UNITS - 1:
                nc.sync.dma_start(out=out_rows[proj][0][b][:, j, :], in_=results[:, 0, :])
                late_stores.append((out_rows[proj][1][b][:, j, :], results[:, 1, :]))

        for slot in range(MX_LAG):
            quantise(slot, transpose_in(slot, vector_is_idle=True))
        spread_bias()
        first_k_finish = UNITS // 2 + BACK_LAG
        for slot in range(MX_LAG, UNITS + BACK_LAG):
            if slot < len(blocks):
                quantise(slot, transpose_in(slot, vector_is_idle=(slot < BACK_LAG)))
            if slot - MX_LAG < UNITS:
                multiply(slot - MX_LAG)
            for target, source in late_stores:
                nc.scalar.dma_start(out=target, in_=source)
            late_stores.clear()
            if slot >= BACK_LAG:
                finish(slot - BACK_LAG)
            j = slot - (first_k_finish - 1)
            if 0 <= j < TOKEN_TILES:
                nc.scalar.mul(rot_sb[:, 2, j, :], rot_sb[:, 1, j, :], -1.0)
